import numpy as np
import ml_dtypes


def mxq(x, axis, fmt="e4m3"):
    dtype, down = {"e4m3": (ml_dtypes.float8_e4m3fn, 7), "e5m2": (ml_dtypes.float8_e5m2, 14)}[fmt]
    v = np.moveaxis(np.asarray(x, np.float32).astype(ml_dtypes.bfloat16).astype(np.float64), axis, -1)
    blocks = v.reshape(v.shape[:-1] + (-1, 32))
    amax = np.abs(blocks).max(-1, keepdims=True)
    byte = np.maximum(np.where(amax > 0, np.frexp(amax)[1] - 1 + 127, 0) - down, 1)
    scale = np.exp2(byte - 127.0)
    codes = (blocks / scale).astype(np.float32).astype(dtype).astype(np.float64)
    return np.moveaxis((codes * scale).reshape(v.shape), -1, axis)


WIDE = False


def mx_kscale(k):
    if not WIDE:
        return np.ones(k)
    levels = np.array([10, -10, 5, -5, 0])
    if k % 512:
        return np.exp2(np.random.permutation(np.resize(levels, k // 32))).repeat(32)
    a = np.empty((k // 512, 16))
    for p in range(k // 512):
        a[p, :8] = np.random.permutation(np.resize(levels, 8))
        for g in range(8):
            far = levels[np.abs(levels - a[p, g]) >= 10]
            a[p, g + 8] = far[np.random.randint(len(far))]
    return np.exp2(a.ravel()).repeat(32)


BF16 = ml_dtypes.bfloat16


def bf(x):
    return np.asarray(x, np.float32).astype(BF16)


def f64(x):
    return np.asarray(x).astype(np.float64)


E2M1 = np.array([0.0, 0.5, 1.0, 1.5, 2.0, 3.0, 4.0, 6.0, -0.0, -0.5, -1.0, -1.5, -2.0, -3.0, -4.0, -6.0])


def pack_weight(w, fmt):
    k, n = w.shape
    w = f64(bf(w)).reshape(k // 32, 32, n)
    amax = np.abs(w).max(1)
    if fmt == "e4m3":
        byte = np.frexp(amax)[1] - 1 + 127 - 7
    else:
        mant, ex = np.frexp(amax / 6.0)
        byte = np.where(mant > 0.5, ex, ex - 1) + 127
    byte = np.clip(np.where(amax > 0, byte, 1), 1, 254)
    scaled = (w * np.exp2(127.0 - byte)[:, None, :]).reshape(k, n).astype(np.float32)
    by_word = np.ascontiguousarray(scaled.reshape(k // 512, 128, 4, n).transpose(0, 1, 3, 2))
    if fmt == "e4m3":
        words = by_word.astype(ml_dtypes.float8_e4m3fn).view(np.uint8)
    else:
        c = by_word.astype(ml_dtypes.float4_e2m1fn).view(np.uint8) & 0xF
        words = c[..., 0::2] | (c[..., 1::2] << 4)
    return np.ascontiguousarray(words), np.ascontiguousarray(byte.astype(np.uint8).reshape(k // 512, 16, n))


def unpack_weight(words, scales, fmt):
    g, p, n, _ = words.shape
    if fmt == "e4m3":
        vals = np.ascontiguousarray(words).view(ml_dtypes.float8_e4m3fn).astype(np.float64)
    else:
        nib = np.empty((g, p, n, 4), np.uint8)
        nib[..., 0::2] = words & 0xF
        nib[..., 1::2] = words >> 4
        vals = E2M1[nib]
    vals = vals * np.repeat(np.exp2(scales.astype(np.float64) - 127.0), 8, axis=1)[..., None]
    return vals.transpose(0, 1, 3, 2).reshape(g * 512, n)


B, S, HIDDEN, Q_LORA, NUM_HEADS, QK_NOPE, QK_ROPE, KV_LORA = 2, 256, 2048, 1536, 16, 128, 64, 448
QK_HEAD = QK_NOPE + QK_ROPE


def rotate_half(t):
    d = t.shape[-1] // 2
    return np.concatenate([-t[..., d:], t[..., :d]], axis=-1)


def draw0():
    s, t = mx_kscale(HIDDEN), mx_kscale(Q_LORA)
    x = bf(np.random.standard_normal((B, S, HIDDEN)) * s)
    cos = bf(np.random.uniform(size=(B, S, QK_ROPE)))
    sin = bf(np.random.uniform(size=(B, S, QK_ROPE)))
    Wqa = np.random.standard_normal((Q_LORA, HIDDEN)) / np.sqrt(HIDDEN) * t[:, None] / s
    Wqb = np.random.standard_normal((NUM_HEADS * QK_HEAD, Q_LORA)) / np.sqrt(Q_LORA) / t
    Wkva = np.random.standard_normal((KV_LORA + QK_ROPE, HIDDEN)) / np.sqrt(HIDDEN) / s
    Wqa_words, Wqa_scales = pack_weight(Wqa.T, "e4m3")
    Wqb_words, Wqb_scales = pack_weight(Wqb.T, "e4m3")
    Wkva_words, Wkva_scales = pack_weight(Wkva.T, "e4m3")
    return {"x": x, "cos": cos, "sin": sin, "Wqa_words": Wqa_words, "Wqa_scales": Wqa_scales, "Wqb_words": Wqb_words, "Wqb_scales": Wqb_scales, "Wkva_words": Wkva_words, "Wkva_scales": Wkva_scales}


def core(x, cos, sin, Wqa_words, Wqa_scales, Wqb_words, Wqb_scales, Wkva_words, Wkva_scales):
    b, s, _ = x.shape
    xq = mxq(f64(x), 2, "e4m3")
    qa = xq @ unpack_weight(Wqa_words, Wqa_scales, "e4m3")
    q = (mxq(qa, 2, "e4m3") @ unpack_weight(Wqb_words, Wqb_scales, "e4m3")).reshape(b, s, NUM_HEADS, QK_HEAD)
    q_nope = q[..., :QK_NOPE]
    q_pe = q[..., QK_NOPE:]
    kv = xq @ unpack_weight(Wkva_words, Wkva_scales, "e4m3")
    compressed_kv = kv[..., :KV_LORA]
    k_pe = kv[..., KV_LORA:].reshape(b, s, 1, QK_ROPE)
    c = f64(cos)[:, :, None, :]
    sn = f64(sin)[:, :, None, :]
    q_pe_rot = q_pe * c + rotate_half(q_pe) * sn
    k_pe_rot = k_pe * c + rotate_half(k_pe) * sn
    q_out = np.concatenate([q_nope, q_pe_rot], axis=-1).reshape(b, s, -1)
    k_out = k_pe_rot.reshape(b, s, QK_ROPE)
    return np.concatenate([q_out, k_out, compressed_kv], axis=-1)


def e4m3fn_bytes(y):
    return np.clip(np.asarray(y, np.float64), -448.0, 448.0).astype(np.float32).astype(ml_dtypes.float8_e4m3fn).view(np.uint8)


def e4m3fn_values(b):
    return np.asarray(b, np.uint8).view(ml_dtypes.float8_e4m3fn).astype(np.float64)


def setup_inputs():
    d = draw0()
    x0 = np.asarray(d['x']).astype(np.float64)
    s = (np.max(np.abs(x0), axis=(0, 1), keepdims=True) / 448.0).astype(np.float32)
    out = {}
    for k, v in d.items():
        if k == 'x':
            out['x_bytes'] = e4m3fn_bytes(x0 / s.astype(np.float64))
            out['x_scale'] = s
        else:
            out[k] = v
    return out


def reference(x_bytes, x_scale, cos, sin, Wqa_words, Wqa_scales, Wqb_words, Wqb_scales, Wkva_words, Wkva_scales):
    return core(e4m3fn_values(x_bytes) * x_scale.astype(np.float64), cos, sin, Wqa_words, Wqa_scales, Wqb_words, Wqb_scales, Wkva_words, Wkva_scales)

@@ -1,0 +1,382 @@
+from contextlib import ExitStack
+
+import concourse.mybir as mybir
+from concourse.masks import make_identity
+
+TOKENS, HIDDEN, Q_LORA = 512, 2048, 1536
+HEADS, NOPE, ROPE, KV_LORA = 16, 128, 64, 448
+HEAD = NOPE + ROPE
+Q_COLS = HEADS * HEAD
+KV_COLS = KV_LORA + ROPE
+
+FLOPS = 2 * TOKENS * HIDDEN * (Q_LORA + KV_COLS) + 2 * TOKENS * Q_LORA * Q_COLS
+
+F32 = mybir.dt.float32
+BF16 = mybir.dt.bfloat16
+I32 = mybir.dt.int32
+U32 = mybir.dt.uint32
+U8 = mybir.dt.uint8
+FP8 = mybir.dt.float8_e4m3fn
+FP8X4 = mybir.dt.float8_e4m3fn_x4
+MULT = mybir.AluOpType.mult
+ADD = mybir.AluOpType.add
+
+P = 128
+BANK = 512
+TILES = TOKENS // P
+XG = HIDDEN // 512
+QG = Q_LORA // 512
+HALF = Q_COLS // 2
+
+
+def tile_mlaselfattn_w8_kernel(
+    tc, x_bytes, x_scale, cos, sin, wqa_words, wqa_scales, wqb_words, wqb_scales, wkva_words, wkva_scales, out
+):
+    nc = tc.nc
+    x_rows = x_bytes.rearrange("b s k -> (b s) k")
+    out_rows = out.rearrange("b s c -> (b s) c")
+
+    with ExitStack() as ctx:
+        keep = ctx.enter_context(tc.tile_pool(name="keep", bufs=1))
+        work = ctx.enter_context(tc.tile_pool(name="work", bufs=2))
+        psum_turn = ctx.enter_context(tc.psum_pool(name="psum_turn", bufs=2))
+        psum_acc = ctx.enter_context(tc.psum_pool(name="psum_acc", bufs=6))
+
+        def kept(name, shape, dtype):
+            return keep.tile(shape, dtype, name=name, align_bytes=64)
+
+        xb = [kept("xb%d" % i, [P, HIDDEN], U8) for i in range(TILES)]
+        xv = [kept("xv%d" % i, [P, HIDDEN], BF16) for i in range(TILES)]
+        xg = [kept("xg%d" % i, [P, XG, P, 4], BF16) for i in range(TILES)]
+        xc = [kept("xc%d" % i, [P, XG, P], U32) for i in range(TILES)]
+        xs = [kept("xs%d" % i, [P, XG, P], U8) for i in range(TILES)]
+        qv = [kept("qv%d" % i, [P, QG, BANK], BF16) for i in range(TILES)]
+        qg = [kept("qg%d" % i, [P, QG, P, 4], BF16) for i in range(TILES)]
+        qc = [kept("qc%d" % i, [P, QG, P], U32) for i in range(TILES)]
+        qs = [kept("qs%d" % i, [P, QG, P], U8) for i in range(TILES)]
+        wa = [kept("wa%d" % g, [P, Q_LORA], U32) for g in range(XG)]
+        wb = [kept("wb%d" % g, [P, Q_COLS], U32) for g in range(QG)]
+        wk = kept("wk", [P, XG, KV_COLS], U32)
+        sa = kept("sa", [P, Q_LORA], U8)
+        sb = kept("sb", [P, Q_COLS], U8)
+        sk = kept("sk", [P, KV_COLS], U8)
+        kscale = kept("kscale", [P, XG, 4], F32)
+        cos_sb = kept("cos_sb", [P, TILES, ROPE], BF16)
+        sin_sb = kept("sin_sb", [P, TILES, ROPE], BF16)
+        sin_neg = kept("sin_neg", [P, TILES, ROPE // 2], BF16)
+        ckv = [kept("ckv%d" % i, [P, KV_LORA], F32) for i in range(TILES)]
+        kp = kept("kp", [P, TILES, ROPE], F32)
+        kt = kept("kt", [P, TILES, ROPE], F32)
+        kt2 = kept("kt2", [P, TILES, ROPE], F32)
+        ident = kept("ident", [P, P], F32)
+        warm = kept("warm", [P, 8], F32)
+
+        ctx.enter_context(tc.manual_schedule())
+
+        nc.vector.memset(warm[:], 0.0)
+        nc.vector.memset(sa[:].bitcast(I32), 0)
+        nc.vector.memset(sk[:].bitcast(I32), 0)
+        nc.vector.memset(sb[:].bitcast(I32), 0)
+        make_identity(nc, ident[:])
+
+        def load_x(i):
+            nc.sync.dma_start(out=xb[i][:], in_=x_rows[i * P : (i + 1) * P, :])
+
+        def load_words(tile, words):
+            nc.sync.dma_start(out=tile.bitcast(I32), in_=words.rearrange("p n t -> p (n t)").bitcast(I32))
+
+        def load_planes(tile, scales):
+            groups = scales.shape[0]
+            for q in range(4):
+                nc.sync.dma_start(
+                    out=tile[32 * q : 32 * q + 4 * groups, :].bitcast(I32),
+                    in_=scales[:, 4 * q : 4 * q + 4, :].bitcast(I32),
+                )
+
+        load_x(0)
+        nc.scalar.dma_start(out=kscale[:], in_=x_scale.rearrange("a b (g p t) -> p (a b g) t", p=P, t=4))
+        nc.scalar.copy(out=warm[:, 4:8], in_=warm[:, 0:4])
+        load_planes(sa, wqa_scales)
+        load_x(1)
+        load_words(wa[0][:], wqa_words[0])
+        load_words(wa[1][:], wqa_words[1])
+        load_words(wa[2][:], wqa_words[2])
+        load_x(2)
+        load_words(wa[3][:], wqa_words[3])
+        load_x(3)
+        load_planes(sk, wkva_scales)
+        nc.sync.dma_start(
+            out=wk[:].bitcast(I32),
+            in_=wkva_words.rearrange("g p n t -> p g (n t)").bitcast(I32),
+        )
+        nc.sync.dma_start(out=cos_sb[:], in_=cos.rearrange("b (h p) d -> p (b h) d", p=P))
+        nc.sync.dma_start(out=sin_sb[:], in_=sin.rearrange("b (h p) d -> p (b h) d", p=P))
+        load_planes(sb, wqb_scales)
+        for h in range(2):
+            for g in range(QG):
+                cols = slice(HALF * h, HALF * (h + 1))
+                nc.sync.dma_start(
+                    out=wb[g][:, cols].bitcast(I32),
+                    in_=wqb_words[g, :, cols, :].rearrange("p n t -> p (n t)").bitcast(I32),
+                )
+
+        turned = {}
+        acc = {}
+
+        def cast(i, g, n):
+            cols = slice(512 * g, 512 * (g + n))
+            nc.scalar.copy(out=xv[i][:, cols], in_=xb[i][:, cols].bitcast(FP8))
+
+        def turn(i, g, n):
+            bank = psum_turn.tile([P, 2, 2, P], F32, name="bank")
+            words = xv[i][:].bitcast(F32)
+            for j in range(n):
+                base = 256 * (g + j)
+                for u in range(2):
+                    nc.tensor.transpose(bank[:, j, u, :], words[:, base + u : base + 256 : 2], ident[:])
+                turned[(i, g + j)] = bank[:, j, :, :]
+
+        def widen(i, g):
+            nc.vector.tensor_tensor(
+                out=xg[i][:, g, :, :].rearrange("p r (u e) -> p r u e", e=2),
+                in0=turned[(i, g)].bitcast(BF16).rearrange("p u (r e) -> p r u e", e=2),
+                in1=kscale[:, g, :].rearrange("p (u e) -> p u e", e=2).unsqueeze(1).to_broadcast([P, P, 2, 2]),
+                op=MULT,
+            )
+
+        def quant_x(i, g, n):
+            gs = slice(g, g + n)
+            nc.vector.quantize_mx(
+                out=xc[i][:, gs, :].rearrange("p g r -> p (g r)").bitcast(FP8X4),
+                scales=xs[i][:, gs, :].rearrange("p g r -> p (g r)"),
+                in_=xg[i][:, gs, :, :].rearrange("p g r t -> p (g r t)"),
+            )
+
+        def qa_pass(i, g, n):
+            if g == 0:
+                acc[(i, n)] = psum_acc.tile([P, BANK], F32, name="acc")
+            cols = slice(BANK * n, BANK * (n + 1))
+            nc.tensor.matmul_mx(
+                out=acc[(i, n)][:],
+                lhsT=xc[i][:, g, :].bitcast(FP8X4),
+                lhsT_scale=xs[i][:, g, :],
+                rhs=wa[g][:, cols].bitcast(FP8X4),
+                rhs_scale=sa[4 * g : P, cols],
+                start=(g == 0),
+                stop=(g == XG - 1),
+            )
+
+        def qa_group(i, g):
+            for n in range(QG):
+                qa_pass(i, g, n)
+
+        def qa_bank(i, n):
+            for g in range(XG):
+                qa_pass(i, g, n)
+
+        def round_qa(i, n):
+            nc.scalar.copy(
+                out=qv[i][:, n, :].rearrange("p (u q e) -> p u q e", u=2, e=2),
+                in_=acc[(i, n)][:].rearrange("p (q u e) -> p u q e", u=2, e=2),
+            )
+
+        def turn_qa(i):
+            words = qv[i][:].rearrange("p g c -> p (g c)").bitcast(F32)
+            for first, n in ((0, 2), (2, 1)):
+                bank = psum_turn.tile([P, 2, 2, P], F32, name="bank")
+                for j in range(n):
+                    for u in range(2):
+                        base = 256 * (first + j) + P * u
+                        nc.tensor.transpose(bank[:, j, u, :], words[:, base : base + P], ident[:])
+                nc.scalar.copy(
+                    out=qg[i][:, first : first + n, :, :].rearrange("p g r t -> p (g r t)").bitcast(F32).rearrange("p (g r u) -> p g r u", g=n, u=2),
+                    in_=bank[:, 0:n, :, :].rearrange("p g u r -> p g r u"),
+                )
+
+        def quant_qa(i):
+            for first, n in ((0, 2), (2, 1)):
+                gs = slice(first, first + n)
+                nc.vector.quantize_mx(
+                    out=qc[i][:, gs, :].rearrange("p g r -> p (g r)").bitcast(FP8X4),
+                    scales=qs[i][:, gs, :].rearrange("p g r -> p (g r)"),
+                    in_=qg[i][:, gs, :, :].rearrange("p g r t -> p (g r t)"),
+                )
+
+        def kv(i, first, last):
+            bank = psum_acc.tile([P, BANK], F32, name="acc")
+            for g in range(XG):
+                nc.tensor.matmul_mx(
+                    out=bank[:, first:last],
+                    lhsT=xc[i][:, g, :].bitcast(FP8X4),
+                    lhsT_scale=xs[i][:, g, :],
+                    rhs=wk[:, g, first:last].bitcast(FP8X4),
+                    rhs_scale=sk[4 * g : P, first:last],
+                    start=(g == 0),
+                    stop=(g == XG - 1),
+                )
+            acc[("kv", i, first)] = bank
+
+        def out_kv(i, first, last):
+            bank = acc[("kv", i, first)]
+            end = min(last, KV_LORA)
+            nc.scalar.copy(out=ckv[i][:, first:end], in_=bank[:, first:end])
+            if last > KV_LORA:
+                nc.scalar.copy(out=kp[:, i, :], in_=bank[:, KV_LORA:])
+            nc.sync.dma_start(
+                out=out_rows[i * P : (i + 1) * P, Q_COLS + ROPE + first : Q_COLS + ROPE + end], in_=ckv[i][:, first:end]
+            )
+
+        def rope_k(first, last):
+            rope(
+                kp[:, first:last, :],
+                cos_sb[:, first:last, :],
+                sin_neg[:, first:last, :],
+                sin_sb[:, first:last, ROPE // 2 :],
+                kt[:, first:last, :],
+                kt2[:, first:last, :],
+            )
+            nc.sync.dma_start(
+                out=out_rows[first * P : last * P, Q_COLS : Q_COLS + ROPE].rearrange("(i p) c -> p i c", p=P),
+                in_=kp[:, first:last, :],
+            )
+
+        def rope(pe, c, sn, s2, t1, t2):
+            h = ROPE // 2
+            nc.vector.tensor_tensor(out=t2[:, :, 0:h], in0=pe[:, :, h:], in1=sn, op=MULT)
+            nc.vector.tensor_tensor(out=t2[:, :, h:], in0=pe[:, :, 0:h], in1=s2, op=MULT)
+            nc.vector.tensor_tensor(out=t1, in0=pe, in1=c, op=MULT)
+            nc.vector.tensor_tensor(out=pe, in0=t1, in1=t2, op=ADD)
+
+        def rope_q(i, q, first, last):
+            pe = q[:].rearrange("p (b c) -> p b c", c=ROPE)[:, first:last:3, :]
+            h = pe.shape[1]
+            t1 = work.tile([P, 8, ROPE], F32, name="t1")
+            t2 = work.tile([P, 8, ROPE], F32, name="t2")
+            rope(
+                pe,
+                cos_sb[:, i, :].unsqueeze(1).to_broadcast([P, h, ROPE]),
+                sin_neg[:, i, :].unsqueeze(1).to_broadcast([P, h, ROPE // 2]),
+                sin_sb[:, i, ROPE // 2 :].unsqueeze(1).to_broadcast([P, h, ROPE // 2]),
+                t1[:, 0:h, :],
+                t2[:, 0:h, :],
+            )
+
+        def q_bank(i, n):
+            bank = psum_acc.tile([P, BANK], F32, name="acc")
+            cols = slice(BANK * n, BANK * (n + 1))
+            for g in range(QG):
+                nc.tensor.matmul_mx(
+                    out=bank[:],
+                    lhsT=qc[i][:, g, :].bitcast(FP8X4),
+                    lhsT_scale=qs[i][:, g, :],
+                    rhs=wb[g][:, cols].bitcast(FP8X4),
+                    rhs_scale=sb[4 * g : P, cols],
+                    start=(g == 0),
+                    stop=(g == QG - 1),
+                )
+            return bank
+
+        def q_half(i, h, cuts):
+            q = work.tile([P, HALF], F32, name="q", bufs=4)
+            first = 0
+            for n in range(3):
+                bank = q_bank(i, 3 * h + n)
+                cols = slice(BANK * n, BANK * (n + 1))
+                nc.scalar.copy(out=q[:, cols], in_=bank[:])
+                if n in cuts:
+                    rope_q(i, q, 8 * first + (2 - 8 * first) % 3, 8 * n + 8)
+                    done = slice(BANK * first, BANK * (n + 1))
+                    nc.sync.dma_start(
+                        out=out_rows[i * P : (i + 1) * P, HALF * h + BANK * first : HALF * h + BANK * (n + 1)], in_=q[:, done]
+                    )
+                    first = n + 1
+
+        for g in range(XG):
+            cast(0, g, 1)
+            turn(0, g, 1)
+            widen(0, g)
+            if g:
+                quant_x(0, g - 1, 1)
+        cast(1, 0, 2)
+        cast(1, 2, 2)
+        qa_group(0, 0)
+        turn(1, 0, 2)
+        widen(1, 0)
+        quant_x(0, 3, 1)
+        widen(1, 1)
+        quant_x(1, 0, 1)
+        turn(1, 2, 2)
+        widen(1, 2)
+        quant_x(1, 1, 1)
+        widen(1, 3)
+        cast(2, 0, 2)
+        cast(2, 2, 2)
+        qa_group(0, 1)
+        qa_group(1, 0)
+        qa_group(0, 2)
+        qa_group(1, 1)
+        quant_x(1, 2, 2)
+        qa_group(1, 2)
+        qa_group(0, 3)
+        qa_group(1, 3)
+        turn(2, 0, 2)
+        widen(2, 0)
+        widen(2, 1)
+        turn(2, 2, 2)
+        widen(2, 2)
+        quant_x(2, 0, 2)
+        widen(2, 3)
+        for n in range(QG):
+            round_qa(0, n)
+        cast(3, 0, 2)
+        cast(3, 2, 2)
+        kv(0, 0, KV_COLS)
+        kv(1, 0, KV_COLS)
+        turn(3, 0, 2)
+        widen(3, 0)
+        quant_x(2, 2, 2)
+        widen(3, 1)
+        turn(3, 2, 2)
+        widen(3, 2)
+        quant_x(3, 0, 2)
+        widen(3, 3)
+        for n in range(QG):
+            round_qa(1, n)
+        qa_bank(2, 0)
+        qa_bank(2, 1)
+        qa_bank(2, 2)
+        quant_x(3, 2, 2)
+        out_kv(0, 0, KV_COLS)
+        out_kv(1, 0, KV_COLS)
+        turn_qa(0)
+        quant_qa(0)
+        for n in range(QG):
+            round_qa(2, n)
+        qa_bank(3, 0)
+        qa_bank(3, 1)
+        qa_bank(3, 2)
+        nc.vector.tensor_scalar(out=sin_neg[:], in0=sin_sb[:, :, 0 : ROPE // 2], scalar1=-1.0, scalar2=None, op0=MULT)
+        turn_qa(1)
+        quant_qa(1)
+        for n in range(QG):
+            round_qa(3, n)
+        rope_k(0, 2)
+        q_half(0, 0, (2,))
+        turn_qa(2)
+        quant_qa(2)
+        q_half(0, 1, (2,))
+        turn_qa(3)
+        quant_qa(3)
+        for h in range(2):
+            q_half(1, h, (2,))
+        for h in range(2):
+            q_half(2, h, (2,))
+        for h in range(2):
+            q_half(3, h, (1, 2))
+        kv(2, 0, KV_COLS)
+        out_kv(2, 0, KV_COLS)
+        kv(3, 256, KV_COLS)
+        out_kv(3, 256, KV_COLS)
+        kv(3, 0, 256)
+        rope_k(2, 4)
+        out_kv(3, 0, 256)

@@ -39,14 +39,17 @@ def tile_mlaselfattn_w8_kernel(
     with ExitStack() as ctx:
         keep = ctx.enter_context(tc.tile_pool(name="keep", bufs=1))
         work = ctx.enter_context(tc.tile_pool(name="work", bufs=2))
-        psum_turn = ctx.enter_context(tc.psum_pool(name="psum_turn", bufs=2))
-        psum_acc = ctx.enter_context(tc.psum_pool(name="psum_acc", bufs=6))
+        psum = ctx.enter_context(tc.psum_pool(name="psum", bufs=8))
+
+        def bank_tile():
+            return psum.tile([P, BANK], F32, name="bank")
 
         def kept(name, shape, dtype):
             return keep.tile(shape, dtype, name=name, align_bytes=64)
 
         xb = [kept("xb%d" % i, [P, HIDDEN], U8) for i in range(TILES)]
         xv = [kept("xv%d" % i, [P, HIDDEN], BF16) for i in range(TILES)]
+        xp = {i: kept("xp%d" % i, [P, XG, 2, P], F32) for i in (2, 3)}
         xg = [kept("xg%d" % i, [P, XG, P, 4], BF16) for i in range(TILES)]
         xc = [kept("xc%d" % i, [P, XG, P], U32) for i in range(TILES)]
         xs = [kept("xs%d" % i, [P, XG, P], U8) for i in range(TILES)]
@@ -70,10 +73,12 @@ def tile_mlaselfattn_w8_kernel(
         kt2 = kept("kt2", [P, TILES, ROPE], F32)
         ident = kept("ident", [P, P], F32)
         warm = kept("warm", [P, 8], F32)
+        zeros = kept("zeros", [P, P + BANK], BF16)
 
         ctx.enter_context(tc.manual_schedule())
 
         nc.vector.memset(warm[:], 0.0)
+        nc.vector.memset(zeros[:], 0.0)
         nc.vector.memset(sa[:].bitcast(I32), 0)
         nc.vector.memset(sk[:].bitcast(I32), 0)
         nc.vector.memset(sb[:].bitcast(I32), 0)
@@ -100,10 +105,10 @@ def tile_mlaselfattn_w8_kernel(
         load_x(1)
         load_words(wa[0][:], wqa_words[0])
         load_words(wa[1][:], wqa_words[1])
-        load_words(wa[2][:], wqa_words[2])
         load_x(2)
-        load_words(wa[3][:], wqa_words[3])
+        load_words(wa[2][:], wqa_words[2])
         load_x(3)
+        load_words(wa[3][:], wqa_words[3])
         load_planes(sk, wkva_scales)
         nc.sync.dma_start(
             out=wk[:].bitcast(I32),
@@ -127,14 +132,24 @@ def tile_mlaselfattn_w8_kernel(
             cols = slice(512 * g, 512 * (g + n))
             nc.scalar.copy(out=xv[i][:, cols], in_=xb[i][:, cols].bitcast(FP8))
 
+        def spread(i):
+            nc.vector.tensor_copy(
+                out=xp[i][:], in_=xv[i][:].bitcast(F32).rearrange("p (g q u) -> p g u q", g=XG, u=2)
+            )
+
         def turn(i, g, n):
-            bank = psum_turn.tile([P, 2, 2, P], F32, name="bank")
+            bank = bank_tile()[:].rearrange("p (j u r) -> p j u r", j=2, u=2)
             words = xv[i][:].bitcast(F32)
             for j in range(n):
                 base = 256 * (g + j)
                 for u in range(2):
-                    nc.tensor.transpose(bank[:, j, u, :], words[:, base + u : base + 256 : 2], ident[:])
+                    source = xp[i][:, g + j, u, :] if i in xp else words[:, base + u : base + 256 : 2]
+                    nc.tensor.transpose(bank[:, j, u, :], source, ident[:])
                 turned[(i, g + j)] = bank[:, j, :, :]
+
+        def keep_warm(bank, n):
+            for j in range(n):
+                nc.tensor.matmul(bank[:], lhsT=zeros[:, 0:P], rhs=zeros[:, P:], start=True, stop=True)
 
         def widen(i, g):
             nc.vector.tensor_tensor(
@@ -154,7 +169,7 @@ def tile_mlaselfattn_w8_kernel(
 
         def qa_pass(i, g, n):
             if g == 0:
-                acc[(i, n)] = psum_acc.tile([P, BANK], F32, name="acc")
+                acc[(i, n)] = bank_tile()
             cols = slice(BANK * n, BANK * (n + 1))
             nc.tensor.matmul_mx(
                 out=acc[(i, n)][:],
@@ -183,7 +198,7 @@ def tile_mlaselfattn_w8_kernel(
         def turn_qa(i):
             words = qv[i][:].rearrange("p g c -> p (g c)").bitcast(F32)
             for first, n in ((0, 2), (2, 1)):
-                bank = psum_turn.tile([P, 2, 2, P], F32, name="bank")
+                bank = bank_tile()[:].rearrange("p (j u r) -> p j u r", j=2, u=2)
                 for j in range(n):
                     for u in range(2):
                         base = 256 * (first + j) + P * u
@@ -203,7 +218,7 @@ def tile_mlaselfattn_w8_kernel(
                 )
 
         def kv(i, first, last):
-            bank = psum_acc.tile([P, BANK], F32, name="acc")
+            bank = bank_tile()
             for g in range(XG):
                 nc.tensor.matmul_mx(
                     out=bank[:, first:last],
@@ -262,7 +277,7 @@ def tile_mlaselfattn_w8_kernel(
             )
 
         def q_bank(i, n):
-            bank = psum_acc.tile([P, BANK], F32, name="acc")
+            bank = bank_tile()
             cols = slice(BANK * n, BANK * (n + 1))
             for g in range(QG):
                 nc.tensor.matmul_mx(
@@ -291,9 +306,12 @@ def tile_mlaselfattn_w8_kernel(
                     )
                     first = n + 1
 
+        idle = bank_tile()
+        keep_warm(idle, 5)
         for g in range(XG):
             cast(0, g, 1)
             turn(0, g, 1)
+            keep_warm(idle, 1)
             widen(0, g)
             if g:
                 quant_x(0, g - 1, 1)
@@ -309,16 +327,20 @@ def tile_mlaselfattn_w8_kernel(
         widen(1, 2)
         quant_x(1, 1, 1)
         widen(1, 3)
-        cast(2, 0, 2)
-        cast(2, 2, 2)
+        cast(2, 0, 4)
+        cast(3, 0, 4)
         qa_group(0, 1)
         qa_group(1, 0)
         qa_group(0, 2)
         qa_group(1, 1)
         quant_x(1, 2, 2)
+        spread(2)
+        spread(3)
         qa_group(1, 2)
         qa_group(0, 3)
         qa_group(1, 3)
+        for n in range(QG):
+            round_qa(0, n)
         turn(2, 0, 2)
         widen(2, 0)
         widen(2, 1)
@@ -326,12 +348,6 @@ def tile_mlaselfattn_w8_kernel(
         widen(2, 2)
         quant_x(2, 0, 2)
         widen(2, 3)
-        for n in range(QG):
-            round_qa(0, n)
-        cast(3, 0, 2)
-        cast(3, 2, 2)
-        kv(0, 0, KV_COLS)
-        kv(1, 0, KV_COLS)
         turn(3, 0, 2)
         widen(3, 0)
         quant_x(2, 2, 2)
@@ -342,33 +358,34 @@ def tile_mlaselfattn_w8_kernel(
         widen(3, 3)
         for n in range(QG):
             round_qa(1, n)
-        qa_bank(2, 0)
-        qa_bank(2, 1)
-        qa_bank(2, 2)
-        quant_x(3, 2, 2)
+        kv(0, 0, KV_COLS)
+        kv(1, 0, KV_COLS)
         out_kv(0, 0, KV_COLS)
         out_kv(1, 0, KV_COLS)
+        quant_x(3, 2, 2)
+        for g in range(XG):
+            qa_group(2, g)
+        nc.vector.tensor_scalar(out=sin_neg[:], in0=sin_sb[:, :, 0 : ROPE // 2], scalar1=-1.0, scalar2=None, op0=MULT)
+        qa_bank(3, 0)
         turn_qa(0)
         quant_qa(0)
-        for n in range(QG):
-            round_qa(2, n)
-        qa_bank(3, 0)
-        qa_bank(3, 1)
-        qa_bank(3, 2)
-        nc.vector.tensor_scalar(out=sin_neg[:], in0=sin_sb[:, :, 0 : ROPE // 2], scalar1=-1.0, scalar2=None, op0=MULT)
         turn_qa(1)
         quant_qa(1)
+        for n in range(QG):
+            round_qa(2, n)
+        qa_bank(3, 1)
+        qa_bank(3, 2)
         for n in range(QG):
             round_qa(3, n)
         rope_k(0, 2)
         q_half(0, 0, (2,))
+        q_half(1, 0, (2,))
         turn_qa(2)
         quant_qa(2)
-        q_half(0, 1, (2,))
         turn_qa(3)
         quant_qa(3)
-        for h in range(2):
-            q_half(1, h, (2,))
+        q_half(0, 1, (2,))
+        q_half(1, 1, (2,))
         for h in range(2):
             q_half(2, h, (2,))
         for h in range(2):

@@ -120,21 +120,19 @@ def tile_mlaselfattn_w8_kernel(
         for h in range(2):
             for g in range(QG):
                 cols = slice(HALF * h, HALF * (h + 1))
-                nc.sync.dma_start(
-                    out=wb[g][:, cols].bitcast(I32),
-                    in_=wqb_words[g, :, cols, :].rearrange("p n t -> p (n t)").bitcast(I32),
-                )
+                load_words(wb[g][:, cols], wqb_words[g, :, cols, :])
 
         turned = {}
         acc = {}
 
-        def cast(i, g, n):
+        def cast(i, g, n, copy=nc.scalar.copy):
             cols = slice(512 * g, 512 * (g + n))
-            nc.scalar.copy(out=xv[i][:, cols], in_=xb[i][:, cols].bitcast(FP8))
+            copy(out=xv[i][:, cols], in_=xb[i][:, cols].bitcast(FP8))
 
-        def spread(i):
+        def spread(i, g, n):
+            words = xv[i][:, 512 * g : 512 * (g + n)].bitcast(F32)
             nc.vector.tensor_copy(
-                out=xp[i][:], in_=xv[i][:].bitcast(F32).rearrange("p (g q u) -> p g u q", g=XG, u=2)
+                out=xp[i][:, g : g + n, :, :], in_=words.rearrange("p (g q u) -> p g u q", g=n, u=2)
             )
 
         def turn(i, g, n):
@@ -308,76 +306,80 @@ def tile_mlaselfattn_w8_kernel(
 
         idle = bank_tile()
         keep_warm(idle, 5)
+        cast(0, 0, 1)
+        cast(0, 1, 1, nc.vector.tensor_copy)
+        cast(0, 2, 1)
+        cast(0, 3, 1)
         for g in range(XG):
-            cast(0, g, 1)
             turn(0, g, 1)
-            keep_warm(idle, 1)
+            if g < 2:
+                keep_warm(idle, 1)
             widen(0, g)
             if g:
                 quant_x(0, g - 1, 1)
         cast(1, 0, 2)
         cast(1, 2, 2)
-        qa_group(0, 0)
         turn(1, 0, 2)
+        qa_group(0, 0)
         widen(1, 0)
         quant_x(0, 3, 1)
         widen(1, 1)
         quant_x(1, 0, 1)
         turn(1, 2, 2)
+        cast(2, 0, 2)
         widen(1, 2)
         quant_x(1, 1, 1)
-        widen(1, 3)
-        cast(2, 0, 4)
-        cast(3, 0, 4)
+        cast(2, 2, 2)
         qa_group(0, 1)
         qa_group(1, 0)
-        qa_group(0, 2)
-        qa_group(1, 1)
+        widen(1, 3)
+        spread(2, 0, 2)
         quant_x(1, 2, 2)
-        spread(2)
-        spread(3)
-        qa_group(1, 2)
-        qa_group(0, 3)
-        qa_group(1, 3)
-        for n in range(QG):
-            round_qa(0, n)
+        spread(2, 2, 2)
+        qa_group(1, 1)
+        qa_group(0, 2)
         turn(2, 0, 2)
+        turn(2, 2, 2)
         widen(2, 0)
         widen(2, 1)
-        turn(2, 2, 2)
+        cast(3, 0, 2)
+        cast(3, 2, 2)
+        qa_group(1, 2)
+        qa_group(0, 3)
+        spread(3, 0, 2)
         widen(2, 2)
+        spread(3, 2, 2)
         quant_x(2, 0, 2)
         widen(2, 3)
-        turn(3, 0, 2)
-        widen(3, 0)
         quant_x(2, 2, 2)
-        widen(3, 1)
+        for n in range(QG):
+            round_qa(0, n)
+        qa_group(1, 3)
+        turn(3, 0, 2)
         turn(3, 2, 2)
+        for n in range(QG):
+            round_qa(1, n)
+        widen(3, 0)
+        widen(3, 1)
+        for n in range(QG):
+            qa_bank(2, n)
         widen(3, 2)
         quant_x(3, 0, 2)
         widen(3, 3)
-        for n in range(QG):
-            round_qa(1, n)
-        kv(0, 0, KV_COLS)
-        kv(1, 0, KV_COLS)
-        out_kv(0, 0, KV_COLS)
-        out_kv(1, 0, KV_COLS)
-        quant_x(3, 2, 2)
-        for g in range(XG):
-            qa_group(2, g)
-        nc.vector.tensor_scalar(out=sin_neg[:], in0=sin_sb[:, :, 0 : ROPE // 2], scalar1=-1.0, scalar2=None, op0=MULT)
-        qa_bank(3, 0)
         turn_qa(0)
-        quant_qa(0)
+        quant_x(3, 2, 2)
         turn_qa(1)
+        quant_qa(0)
         quant_qa(1)
         for n in range(QG):
             round_qa(2, n)
-        qa_bank(3, 1)
-        qa_bank(3, 2)
+        kv(0, 0, KV_COLS)
+        out_kv(0, 0, KV_COLS)
+        nc.vector.tensor_scalar(out=sin_neg[:], in0=sin_sb[:, :, 0 : ROPE // 2], scalar1=-1.0, scalar2=None, op0=MULT)
+        for n in range(QG):
+            qa_bank(3, n)
         for n in range(QG):
             round_qa(3, n)
-        rope_k(0, 2)
         q_half(0, 0, (2,))
         q_half(1, 0, (2,))
         turn_qa(2)
@@ -390,10 +392,9 @@ def tile_mlaselfattn_w8_kernel(
             q_half(2, h, (2,))
         for h in range(2):
             q_half(3, h, (1, 2))
-        kv(2, 0, KV_COLS)
-        out_kv(2, 0, KV_COLS)
-        kv(3, 256, KV_COLS)
-        out_kv(3, 256, KV_COLS)
-        kv(3, 0, 256)
-        rope_k(2, 4)
-        out_kv(3, 0, 256)
+        for first in (256, 0):
+            for i in range(1, TILES):
+                kv(i, first, first + 256)
+                out_kv(i, first, first + 256)
+            if first:
+                rope_k(0, TILES)

@@ -114,10 +114,11 @@ def tile_mlaselfattn_w8_kernel(
             out=wk[:].bitcast(I32),
             in_=wkva_words.rearrange("g p n t -> p g (n t)").bitcast(I32),
         )
-        nc.sync.dma_start(out=cos_sb[:], in_=cos.rearrange("b (h p) d -> p (b h) d", p=P))
-        nc.sync.dma_start(out=sin_sb[:], in_=sin.rearrange("b (h p) d -> p (b h) d", p=P))
         load_planes(sb, wqb_scales)
         for h in range(2):
+            if h:
+                nc.sync.dma_start(out=cos_sb[:], in_=cos.rearrange("b (h p) d -> p (b h) d", p=P))
+                nc.sync.dma_start(out=sin_sb[:], in_=sin.rearrange("b (h p) d -> p (b h) d", p=P))
             for g in range(QG):
                 cols = slice(HALF * h, HALF * (h + 1))
                 load_words(wb[g][:, cols], wqb_words[g, :, cols, :])
@@ -125,8 +126,8 @@ def tile_mlaselfattn_w8_kernel(
         turned = {}
         acc = {}
 
-        def cast(i, g, n, copy=nc.scalar.copy):
-            cols = slice(512 * g, 512 * (g + n))
+        def cast(i, first, last, copy=nc.scalar.copy):
+            cols = slice(512 * first // 2, 512 * last // 2)
             copy(out=xv[i][:, cols], in_=xb[i][:, cols].bitcast(FP8))
 
         def spread(i, g, n):
@@ -235,9 +236,13 @@ def tile_mlaselfattn_w8_kernel(
             nc.scalar.copy(out=ckv[i][:, first:end], in_=bank[:, first:end])
             if last > KV_LORA:
                 nc.scalar.copy(out=kp[:, i, :], in_=bank[:, KV_LORA:])
-            nc.sync.dma_start(
+            nc.scalar.dma_start(
                 out=out_rows[i * P : (i + 1) * P, Q_COLS + ROPE + first : Q_COLS + ROPE + end], in_=ckv[i][:, first:end]
             )
+
+        def kv_part(i, first):
+            kv(i, first, first + 256)
+            out_kv(i, first, first + 256)
 
         def rope_k(first, last):
             rope(
@@ -260,8 +265,8 @@ def tile_mlaselfattn_w8_kernel(
             nc.vector.tensor_tensor(out=t1, in0=pe, in1=c, op=MULT)
             nc.vector.tensor_tensor(out=pe, in0=t1, in1=t2, op=ADD)
 
-        def rope_q(i, q, first, last):
-            pe = q[:].rearrange("p (b c) -> p b c", c=ROPE)[:, first:last:3, :]
+        def rope_q(i, q, first):
+            pe = q[:].rearrange("p (b c) -> p b c", c=ROPE)[:, first::3, :]
             h = pe.shape[1]
             t1 = work.tile([P, 8, ROPE], F32, name="t1")
             t2 = work.tile([P, 8, ROPE], F32, name="t2")
@@ -289,27 +294,21 @@ def tile_mlaselfattn_w8_kernel(
                 )
             return bank
 
-        def q_half(i, h, cuts):
-            q = work.tile([P, HALF], F32, name="q", bufs=4)
-            first = 0
-            for n in range(3):
-                bank = q_bank(i, 3 * h + n)
-                cols = slice(BANK * n, BANK * (n + 1))
-                nc.scalar.copy(out=q[:, cols], in_=bank[:])
-                if n in cuts:
-                    rope_q(i, q, 8 * first + (2 - 8 * first) % 3, 8 * n + 8)
-                    done = slice(BANK * first, BANK * (n + 1))
-                    nc.sync.dma_start(
-                        out=out_rows[i * P : (i + 1) * P, HALF * h + BANK * first : HALF * h + BANK * (n + 1)], in_=q[:, done]
-                    )
-                    first = n + 1
+        def q_part(i, first, n):
+            q = work.tile([P, n * BANK], F32, name="q%d" % n, bufs=4)
+            for j in range(n):
+                bank = q_bank(i, first + j)
+                nc.scalar.copy(out=q[:, BANK * j : BANK * (j + 1)], in_=bank[:])
+            rope_q(i, q, (2 - 8 * first) % 3)
+            nc.sync.dma_start(out=out_rows[i * P : (i + 1) * P, BANK * first : BANK * (first + n)], in_=q[:])
 
         idle = bank_tile()
         keep_warm(idle, 5)
         cast(0, 0, 1)
-        cast(0, 1, 1, nc.vector.tensor_copy)
-        cast(0, 2, 1)
-        cast(0, 3, 1)
+        cast(0, 1, 2, nc.vector.tensor_copy)
+        cast(0, 2, 4)
+        cast(0, 4, 6, nc.vector.tensor_copy)
+        cast(0, 6, 8)
         for g in range(XG):
             turn(0, g, 1)
             if g < 2:
@@ -317,8 +316,8 @@ def tile_mlaselfattn_w8_kernel(
             widen(0, g)
             if g:
                 quant_x(0, g - 1, 1)
-        cast(1, 0, 2)
-        cast(1, 2, 2)
+        cast(1, 0, 4)
+        cast(1, 4, 8)
         turn(1, 0, 2)
         qa_group(0, 0)
         widen(1, 0)
@@ -326,10 +325,10 @@ def tile_mlaselfattn_w8_kernel(
         widen(1, 1)
         quant_x(1, 0, 1)
         turn(1, 2, 2)
-        cast(2, 0, 2)
+        cast(2, 0, 4)
         widen(1, 2)
         quant_x(1, 1, 1)
-        cast(2, 2, 2)
+        cast(2, 4, 8)
         qa_group(0, 1)
         qa_group(1, 0)
         widen(1, 3)
@@ -342,8 +341,8 @@ def tile_mlaselfattn_w8_kernel(
         turn(2, 2, 2)
         widen(2, 0)
         widen(2, 1)
-        cast(3, 0, 2)
-        cast(3, 2, 2)
+        cast(3, 0, 4)
+        cast(3, 4, 8)
         qa_group(1, 2)
         qa_group(0, 3)
         spread(3, 0, 2)
@@ -361,8 +360,8 @@ def tile_mlaselfattn_w8_kernel(
             round_qa(1, n)
         widen(3, 0)
         widen(3, 1)
-        for n in range(QG):
-            qa_bank(2, n)
+        for g in range(XG):
+            qa_group(2, g)
         widen(3, 2)
         quant_x(3, 0, 2)
         widen(3, 3)
@@ -373,28 +372,25 @@ def tile_mlaselfattn_w8_kernel(
         quant_qa(1)
         for n in range(QG):
             round_qa(2, n)
-        kv(0, 0, KV_COLS)
-        out_kv(0, 0, KV_COLS)
         nc.vector.tensor_scalar(out=sin_neg[:], in0=sin_sb[:, :, 0 : ROPE // 2], scalar1=-1.0, scalar2=None, op0=MULT)
         for n in range(QG):
             qa_bank(3, n)
         for n in range(QG):
             round_qa(3, n)
-        q_half(0, 0, (2,))
-        q_half(1, 0, (2,))
+        q_part(0, 0, 3)
+        q_part(1, 0, 3)
         turn_qa(2)
         quant_qa(2)
         turn_qa(3)
         quant_qa(3)
-        q_half(0, 1, (2,))
-        q_half(1, 1, (2,))
-        for h in range(2):
-            q_half(2, h, (2,))
-        for h in range(2):
-            q_half(3, h, (1, 2))
-        for first in (256, 0):
-            for i in range(1, TILES):
-                kv(i, first, first + 256)
-                out_kv(i, first, first + 256)
-            if first:
-                rope_k(0, TILES)
+        q_part(0, 3, 3)
+        q_part(1, 3, 3)
+        q_part(2, 0, 3)
+        q_part(2, 3, 3)
+        q_part(3, 0, 3)
+        q_part(3, 3, 3)
+        for i in range(TILES):
+            kv_part(i, 256)
+        rope_k(0, 4)
+        for i in range(TILES):
+            kv_part(i, 0)

from contextlib import ExitStack

import concourse.mybir as mybir
from concourse.masks import make_identity

TOKENS, HIDDEN, Q_LORA = 512, 2048, 1536
HEADS, NOPE, ROPE, KV_LORA = 16, 128, 64, 448
HEAD = NOPE + ROPE
Q_COLS = HEADS * HEAD
KV_COLS = KV_LORA + ROPE

FLOPS = 2 * TOKENS * HIDDEN * (Q_LORA + KV_COLS) + 2 * TOKENS * Q_LORA * Q_COLS

F32 = mybir.dt.float32
BF16 = mybir.dt.bfloat16
I32 = mybir.dt.int32
U32 = mybir.dt.uint32
U8 = mybir.dt.uint8
FP8 = mybir.dt.float8_e4m3fn
FP8X4 = mybir.dt.float8_e4m3fn_x4
MULT = mybir.AluOpType.mult
ADD = mybir.AluOpType.add

P = 128
BANK = 512
TILES = TOKENS // P
XG = HIDDEN // 512
QG = Q_LORA // 512
HALF = Q_COLS // 2


def tile_mlaselfattn_w8_kernel(
    tc, x_bytes, x_scale, cos, sin, wqa_words, wqa_scales, wqb_words, wqb_scales, wkva_words, wkva_scales, out
):
    nc = tc.nc
    x_rows = x_bytes.rearrange("b s k -> (b s) k")
    out_rows = out.rearrange("b s c -> (b s) c")

    with ExitStack() as ctx:
        keep = ctx.enter_context(tc.tile_pool(name="keep", bufs=1))
        work = ctx.enter_context(tc.tile_pool(name="work", bufs=2))
        psum = ctx.enter_context(tc.psum_pool(name="psum", bufs=8))

        def bank_tile():
            return psum.tile([P, BANK], F32, name="bank")

        def kept(name, shape, dtype):
            return keep.tile(shape, dtype, name=name, align_bytes=64)

        xb = [kept("xb%d" % i, [P, HIDDEN], U8) for i in range(TILES)]
        xv = [kept("xv%d" % i, [P, HIDDEN], BF16) for i in range(TILES)]
        xp = {i: kept("xp%d" % i, [P, XG, 2, P], F32) for i in (2, 3)}
        xg = [kept("xg%d" % i, [P, XG, P, 4], BF16) for i in range(TILES)]
        xc = [kept("xc%d" % i, [P, XG, P], U32) for i in range(TILES)]
        xs = [kept("xs%d" % i, [P, XG, P], U8) for i in range(TILES)]
        qv = [kept("qv%d" % i, [P, QG, BANK], BF16) for i in range(TILES)]
        qg = [kept("qg%d" % i, [P, QG, P, 4], BF16) for i in range(TILES)]
        qc = [kept("qc%d" % i, [P, QG, P], U32) for i in range(TILES)]
        qs = [kept("qs%d" % i, [P, QG, P], U8) for i in range(TILES)]
        wa = [kept("wa%d" % g, [P, Q_LORA], U32) for g in range(XG)]
        wb = [kept("wb%d" % g, [P, Q_COLS], U32) for g in range(QG)]
        wk = kept("wk", [P, XG, KV_COLS], U32)
        sa = kept("sa", [P, Q_LORA], U8)
        sb = kept("sb", [P, Q_COLS], U8)
        sk = kept("sk", [P, KV_COLS], U8)
        kscale = kept("kscale", [P, XG, 4], F32)
        cos_sb = kept("cos_sb", [P, TILES, ROPE], BF16)
        sin_sb = kept("sin_sb", [P, TILES, ROPE], BF16)
        sin_neg = kept("sin_neg", [P, TILES, ROPE // 2], BF16)
        ckv = [kept("ckv%d" % i, [P, KV_LORA], F32) for i in range(TILES)]
        kp = kept("kp", [P, TILES, ROPE], F32)
        kt = kept("kt", [P, TILES, ROPE], F32)
        kt2 = kept("kt2", [P, TILES, ROPE], F32)
        ident = kept("ident", [P, P], F32)
        warm = kept("warm", [P, 8], F32)
        zeros = kept("zeros", [P, P + BANK], BF16)

        ctx.enter_context(tc.manual_schedule())

        nc.vector.memset(warm[:], 0.0)
        nc.vector.memset(zeros[:], 0.0)
        nc.vector.memset(sa[:].bitcast(I32), 0)
        nc.vector.memset(sk[:].bitcast(I32), 0)
        nc.vector.memset(sb[:].bitcast(I32), 0)
        make_identity(nc, ident[:])

        def load_x(i):
            nc.sync.dma_start(out=xb[i][:], in_=x_rows[i * P : (i + 1) * P, :])

        def load_words(tile, words):
            nc.sync.dma_start(out=tile.bitcast(I32), in_=words.rearrange("p n t -> p (n t)").bitcast(I32))

        def load_planes(tile, scales):
            groups = scales.shape[0]
            for q in range(4):
                nc.sync.dma_start(
                    out=tile[32 * q : 32 * q + 4 * groups, :].bitcast(I32),
                    in_=scales[:, 4 * q : 4 * q + 4, :].bitcast(I32),
                )

        load_x(0)
        nc.scalar.dma_start(out=kscale[:], in_=x_scale.rearrange("a b (g p t) -> p (a b g) t", p=P, t=4))
        nc.scalar.copy(out=warm[:, 4:8], in_=warm[:, 0:4])
        load_planes(sa, wqa_scales)
        load_x(1)
        load_words(wa[0][:], wqa_words[0])
        load_words(wa[1][:], wqa_words[1])
        load_x(2)
        load_words(wa[2][:], wqa_words[2])
        load_x(3)
        load_words(wa[3][:], wqa_words[3])
        load_planes(sk, wkva_scales)
        nc.sync.dma_start(
            out=wk[:].bitcast(I32),
            in_=wkva_words.rearrange("g p n t -> p g (n t)").bitcast(I32),
        )
        load_planes(sb, wqb_scales)
        for h in range(2):
            if h:
                nc.sync.dma_start(out=cos_sb[:], in_=cos.rearrange("b (h p) d -> p (b h) d", p=P))
                nc.sync.dma_start(out=sin_sb[:], in_=sin.rearrange("b (h p) d -> p (b h) d", p=P))
            for g in range(QG):
                cols = slice(HALF * h, HALF * (h + 1))
                load_words(wb[g][:, cols], wqb_words[g, :, cols, :])

        turned = {}
        acc = {}

        def cast(i, first, last, copy=nc.scalar.copy):
            cols = slice(512 * first // 2, 512 * last // 2)
            copy(out=xv[i][:, cols], in_=xb[i][:, cols].bitcast(FP8))

        def spread(i, g, n):
            words = xv[i][:, 512 * g : 512 * (g + n)].bitcast(F32)
            nc.vector.tensor_copy(
                out=xp[i][:, g : g + n, :, :], in_=words.rearrange("p (g q u) -> p g u q", g=n, u=2)
            )

        def turn(i, g, n):
            bank = bank_tile()[:].rearrange("p (j u r) -> p j u r", j=2, u=2)
            words = xv[i][:].bitcast(F32)
            for j in range(n):
                base = 256 * (g + j)
                for u in range(2):
                    source = xp[i][:, g + j, u, :] if i in xp else words[:, base + u : base + 256 : 2]
                    nc.tensor.transpose(bank[:, j, u, :], source, ident[:])
                turned[(i, g + j)] = bank[:, j, :, :]

        def keep_warm(bank, n):
            for j in range(n):
                nc.tensor.matmul(bank[:], lhsT=zeros[:, 0:P], rhs=zeros[:, P:], start=True, stop=True)

        def widen(i, g):
            nc.vector.tensor_tensor(
                out=xg[i][:, g, :, :].rearrange("p r (u e) -> p r u e", e=2),
                in0=turned[(i, g)].bitcast(BF16).rearrange("p u (r e) -> p r u e", e=2),
                in1=kscale[:, g, :].rearrange("p (u e) -> p u e", e=2).unsqueeze(1).to_broadcast([P, P, 2, 2]),
                op=MULT,
            )

        def quant_x(i, g, n):
            gs = slice(g, g + n)
            nc.vector.quantize_mx(
                out=xc[i][:, gs, :].rearrange("p g r -> p (g r)").bitcast(FP8X4),
                scales=xs[i][:, gs, :].rearrange("p g r -> p (g r)"),
                in_=xg[i][:, gs, :, :].rearrange("p g r t -> p (g r t)"),
            )

        def qa_pass(i, g, n):
            if g == 0:
                acc[(i, n)] = bank_tile()
            cols = slice(BANK * n, BANK * (n + 1))
            nc.tensor.matmul_mx(
                out=acc[(i, n)][:],
                lhsT=xc[i][:, g, :].bitcast(FP8X4),
                lhsT_scale=xs[i][:, g, :],
                rhs=wa[g][:, cols].bitcast(FP8X4),
                rhs_scale=sa[4 * g : P, cols],
                start=(g == 0),
                stop=(g == XG - 1),
            )

        def qa_group(i, g):
            for n in range(QG):
                qa_pass(i, g, n)

        def qa_bank(i, n):
            for g in range(XG):
                qa_pass(i, g, n)

        def round_qa(i, n):
            nc.scalar.copy(
                out=qv[i][:, n, :].rearrange("p (u q e) -> p u q e", u=2, e=2),
                in_=acc[(i, n)][:].rearrange("p (q u e) -> p u q e", u=2, e=2),
            )

        def turn_qa(i):
            words = qv[i][:].rearrange("p g c -> p (g c)").bitcast(F32)
            for first, n in ((0, 2), (2, 1)):
                bank = bank_tile()[:].rearrange("p (j u r) -> p j u r", j=2, u=2)
                for j in range(n):
                    for u in range(2):
                        base = 256 * (first + j) + P * u
                        nc.tensor.transpose(bank[:, j, u, :], words[:, base : base + P], ident[:])
                nc.scalar.copy(
                    out=qg[i][:, first : first + n, :, :].rearrange("p g r t -> p (g r t)").bitcast(F32).rearrange("p (g r u) -> p g r u", g=n, u=2),
                    in_=bank[:, 0:n, :, :].rearrange("p g u r -> p g r u"),
                )

        def quant_qa(i):
            for first, n in ((0, 2), (2, 1)):
                gs = slice(first, first + n)
                nc.vector.quantize_mx(
                    out=qc[i][:, gs, :].rearrange("p g r -> p (g r)").bitcast(FP8X4),
                    scales=qs[i][:, gs, :].rearrange("p g r -> p (g r)"),
                    in_=qg[i][:, gs, :, :].rearrange("p g r t -> p (g r t)"),
                )

        def kv(i, first, last):
            bank = bank_tile()
            for g in range(XG):
                nc.tensor.matmul_mx(
                    out=bank[:, first:last],
                    lhsT=xc[i][:, g, :].bitcast(FP8X4),
                    lhsT_scale=xs[i][:, g, :],
                    rhs=wk[:, g, first:last].bitcast(FP8X4),
                    rhs_scale=sk[4 * g : P, first:last],
                    start=(g == 0),
                    stop=(g == XG - 1),
                )
            acc[("kv", i, first)] = bank

        def out_kv(i, first, last):
            bank = acc[("kv", i, first)]
            end = min(last, KV_LORA)
            nc.scalar.copy(out=ckv[i][:, first:end], in_=bank[:, first:end])
            if last > KV_LORA:
                nc.scalar.copy(out=kp[:, i, :], in_=bank[:, KV_LORA:])
            nc.scalar.dma_start(
                out=out_rows[i * P : (i + 1) * P, Q_COLS + ROPE + first : Q_COLS + ROPE + end], in_=ckv[i][:, first:end]
            )

        def kv_part(i, first):
            kv(i, first, first + 256)
            out_kv(i, first, first + 256)

        def rope_k(first, last):
            rope(
                kp[:, first:last, :],
                cos_sb[:, first:last, :],
                sin_neg[:, first:last, :],
                sin_sb[:, first:last, ROPE // 2 :],
                kt[:, first:last, :],
                kt2[:, first:last, :],
            )
            nc.sync.dma_start(
                out=out_rows[first * P : last * P, Q_COLS : Q_COLS + ROPE].rearrange("(i p) c -> p i c", p=P),
                in_=kp[:, first:last, :],
            )

        def rope(pe, c, sn, s2, t1, t2):
            h = ROPE // 2
            nc.vector.tensor_tensor(out=t2[:, :, 0:h], in0=pe[:, :, h:], in1=sn, op=MULT)
            nc.vector.tensor_tensor(out=t2[:, :, h:], in0=pe[:, :, 0:h], in1=s2, op=MULT)
            nc.vector.tensor_tensor(out=t1, in0=pe, in1=c, op=MULT)
            nc.vector.tensor_tensor(out=pe, in0=t1, in1=t2, op=ADD)

        def rope_q(i, q, first):
            pe = q[:].rearrange("p (b c) -> p b c", c=ROPE)[:, first::3, :]
            h = pe.shape[1]
            t1 = work.tile([P, 8, ROPE], F32, name="t1")
            t2 = work.tile([P, 8, ROPE], F32, name="t2")
            rope(
                pe,
                cos_sb[:, i, :].unsqueeze(1).to_broadcast([P, h, ROPE]),
                sin_neg[:, i, :].unsqueeze(1).to_broadcast([P, h, ROPE // 2]),
                sin_sb[:, i, ROPE // 2 :].unsqueeze(1).to_broadcast([P, h, ROPE // 2]),
                t1[:, 0:h, :],
                t2[:, 0:h, :],
            )

        def q_bank(i, n):
            bank = bank_tile()
            cols = slice(BANK * n, BANK * (n + 1))
            for g in range(QG):
                nc.tensor.matmul_mx(
                    out=bank[:],
                    lhsT=qc[i][:, g, :].bitcast(FP8X4),
                    lhsT_scale=qs[i][:, g, :],
                    rhs=wb[g][:, cols].bitcast(FP8X4),
                    rhs_scale=sb[4 * g : P, cols],
                    start=(g == 0),
                    stop=(g == QG - 1),
                )
            return bank

        def q_part(i, first, n):
            q = work.tile([P, n * BANK], F32, name="q%d" % n, bufs=4)
            for j in range(n):
                bank = q_bank(i, first + j)
                nc.scalar.copy(out=q[:, BANK * j : BANK * (j + 1)], in_=bank[:])
            rope_q(i, q, (2 - 8 * first) % 3)
            nc.sync.dma_start(out=out_rows[i * P : (i + 1) * P, BANK * first : BANK * (first + n)], in_=q[:])

        idle = bank_tile()
        keep_warm(idle, 5)
        cast(0, 0, 1)
        cast(0, 1, 2, nc.vector.tensor_copy)
        cast(0, 2, 4)
        cast(0, 4, 6, nc.vector.tensor_copy)
        cast(0, 6, 8)
        for g in range(XG):
            turn(0, g, 1)
            if g < 2:
                keep_warm(idle, 1)
            widen(0, g)
            if g:
                quant_x(0, g - 1, 1)
        cast(1, 0, 4)
        cast(1, 4, 8)
        turn(1, 0, 2)
        qa_group(0, 0)
        widen(1, 0)
        quant_x(0, 3, 1)
        widen(1, 1)
        quant_x(1, 0, 1)
        turn(1, 2, 2)
        cast(2, 0, 4)
        widen(1, 2)
        quant_x(1, 1, 1)
        cast(2, 4, 8)
        qa_group(0, 1)
        qa_group(1, 0)
        widen(1, 3)
        spread(2, 0, 2)
        quant_x(1, 2, 2)
        spread(2, 2, 2)
        qa_group(1, 1)
        qa_group(0, 2)
        turn(2, 0, 2)
        turn(2, 2, 2)
        widen(2, 0)
        widen(2, 1)
        cast(3, 0, 4)
        cast(3, 4, 8)
        qa_group(1, 2)
        qa_group(0, 3)
        spread(3, 0, 2)
        widen(2, 2)
        spread(3, 2, 2)
        quant_x(2, 0, 2)
        widen(2, 3)
        quant_x(2, 2, 2)
        for n in range(QG):
            round_qa(0, n)
        qa_group(1, 3)
        turn(3, 0, 2)
        turn(3, 2, 2)
        for n in range(QG):
            round_qa(1, n)
        widen(3, 0)
        widen(3, 1)
        for g in range(XG):
            qa_group(2, g)
        widen(3, 2)
        quant_x(3, 0, 2)
        widen(3, 3)
        turn_qa(0)
        quant_x(3, 2, 2)
        turn_qa(1)
        quant_qa(0)
        quant_qa(1)
        for n in range(QG):
            round_qa(2, n)
        nc.vector.tensor_scalar(out=sin_neg[:], in0=sin_sb[:, :, 0 : ROPE // 2], scalar1=-1.0, scalar2=None, op0=MULT)
        for n in range(QG):
            qa_bank(3, n)
        for n in range(QG):
            round_qa(3, n)
        q_part(0, 0, 3)
        q_part(1, 0, 3)
        turn_qa(2)
        quant_qa(2)
        turn_qa(3)
        quant_qa(3)
        q_part(0, 3, 3)
        q_part(1, 3, 3)
        q_part(2, 0, 3)
        q_part(2, 3, 3)
        q_part(3, 0, 3)
        q_part(3, 3, 3)
        for i in range(TILES):
            kv_part(i, 256)
        rope_k(0, 4)
        for i in range(TILES):
            kv_part(i, 0)
